import numpy as np
import ml_dtypes


def mxq(x, axis, fmt="e4m3"):
    dtype, down = {"e4m3": (ml_dtypes.float8_e4m3fn, 7), "e5m2": (ml_dtypes.float8_e5m2, 14)}[fmt]
    v = np.moveaxis(np.asarray(x, np.float32).astype(ml_dtypes.bfloat16).astype(np.float64), axis, -1)
    blocks = v.reshape(v.shape[:-1] + (-1, 32))
    amax = np.abs(blocks).max(-1, keepdims=True)
    byte = np.maximum(np.where(amax > 0, np.frexp(amax)[1] - 1 + 127, 0) - down, 1)
    scale = np.exp2(byte - 127.0)
    codes = (blocks / scale).astype(np.float32).astype(dtype).astype(np.float64)
    return np.moveaxis((codes * scale).reshape(v.shape), -1, axis)


WIDE = False


def mx_kscale(k):
    if not WIDE:
        return np.ones(k)
    levels = np.array([10, -10, 5, -5, 0])
    a = np.random.permutation(np.resize(levels, k // 512 * 4)).reshape(k // 512, 4)
    idx = np.arange(k)
    return np.exp2(a[idx // 512, idx % 128 // 32])


BF16 = ml_dtypes.bfloat16


def bf(x):
    return np.asarray(x, np.float32).astype(BF16)


def f64(x):
    return np.asarray(x).astype(np.float64)


B, S, D, H = 16, 256, 512, 2


def setup_inputs():
    s = mx_kscale(D)
    t = np.tile(mx_kscale(D), H)
    return {"x": bf(np.random.standard_normal((B, S, D)) * s),
            "Wq": bf(np.random.standard_normal((D, H * D)) * 1.4 / np.sqrt(D) / s[:, None] * t),
            "Wk": bf(np.random.standard_normal((D, H * D)) * 1.4 / np.sqrt(D) / s[:, None] / t)}


def reference(x, Wq, Wk):
    xq = mxq(f64(x), 2, "e4m3")
    Q = np.reshape(xq @ mxq(f64(Wq), 0, "e4m3"), (B, H, S, D))
    K = np.reshape(xq @ mxq(f64(Wk), 0, "e4m3"), (B, H, S, D))
    scores = mxq(Q, 3, "e4m3") @ mxq(K, 3, "e4m3").transpose(0, 1, 3, 2)
    z = scores / np.sqrt(D)
    e = np.exp(z - z.max(-1, keepdims=True))
    return e / e.sum(-1, keepdims=True)

@@ -1,0 +1,196 @@
+import math
+from contextlib import ExitStack
+
+import concourse.mybir as mybir
+from concourse.masks import make_identity
+
+F32 = mybir.dt.float32
+BF16 = mybir.dt.bfloat16
+U32 = mybir.dt.uint32
+U8 = mybir.dt.uint8
+FP8X4 = mybir.dt.float8_e4m3fn_x4
+EXP = mybir.ActivationFunctionType.Exp
+
+P = 128
+PACK = 4
+BATCH, TOKENS, FEATURES, HEADS = 16, 256, 512, 2
+HALVES = 2
+UNITS = BATCH * HEADS
+ROWS = TOKENS
+SOFTMAX_SCALE = 1.0 / math.sqrt(FEATURES)
+
+FLOPS = 2 * 2 * BATCH * TOKENS * FEATURES * HEADS * FEATURES + 2 * UNITS * ROWS * ROWS * FEATURES
+
+
+def tile_bertselfattention_pa_t_kernel(tc, x, Wq, Wk, out):
+    nc = tc.nc
+    with ExitStack() as ctx:
+        keep = ctx.enter_context(tc.tile_pool(name="keep", bufs=1))
+        x_pool = ctx.enter_context(tc.tile_pool(name="x_pool", bufs=BATCH))
+        stage = ctx.enter_context(tc.tile_pool(name="stage", bufs=3))
+        prob_pool = ctx.enter_context(tc.tile_pool(name="prob_pool", bufs=4))
+        psum_x = ctx.enter_context(tc.psum_pool(name="psum_x", bufs=1))
+        psum_proj = ctx.enter_context(tc.psum_pool(name="psum_proj", bufs=5))
+        psum_score = ctx.enter_context(tc.psum_pool(name="psum_score", bufs=2))
+
+        weights = (Wq, Wk)
+        w_raw = []
+        x_rows = []
+        x_view = x.rearrange("b (p two) k -> p b (two k)", two=2)
+
+        def load_weight(w):
+            raw = keep.tile([P, PACK, HEADS * FEATURES], BF16, name="w_raw%d" % w)
+            nc.sync.dma_start(
+                out=raw[:].rearrange("q (u e) c -> q u e c", u=2),
+                in_=weights[w].rearrange("(u q e) c -> q u e c", u=2, e=2),
+            )
+            w_raw.append(raw)
+
+        def load_x(b):
+            rows = x_pool.tile([P, 2 * FEATURES], BF16, name="x_rows")
+            nc.sync.dma_start(out=rows[:], in_=x_view[:, b, :])
+            x_rows.append(rows)
+
+        load_weight(0)
+        load_x(0)
+        load_weight(1)
+        for b in range(1, BATCH):
+            load_x(b)
+
+        identity = keep.tile([P, P], F32, name="identity")
+        make_identity(nc, identity[:])
+
+        zero = keep.tile([P, 1], F32, name="zero")
+        one = keep.tile([P, 1], F32, name="one")
+        nc.vector.memset(zero[:], 0.0)
+        nc.scalar.activation(out=one[:], in_=zero[:], func=EXP)
+
+        w_codes = [keep.tile([P, HEADS * FEATURES], U32, name="w_codes%d" % w, align_bytes=64) for w in range(2)]
+        w_scales = [keep.tile([P, HEADS * FEATURES], U8, name="w_scales%d" % w, align_bytes=64) for w in range(2)]
+        for w in range(2):
+            w_grouped = keep.tile([P, HEADS * FEATURES, PACK], BF16, name="w_grouped%d" % w, align_bytes=64)
+            for half in range(HALVES):
+                cols = slice(FEATURES * half, FEATURES * (half + 1))
+                copy = nc.vector.tensor_copy if half == 0 else nc.scalar.copy
+                copy(out=w_grouped[:, cols, :], in_=w_raw[w][:, :, cols].rearrange("q t c -> q c t"))
+            for half in range(HALVES):
+                cols = slice(FEATURES * half, FEATURES * (half + 1))
+                nc.vector.quantize_mx(
+                    out=w_codes[w][:, cols].bitcast(FP8X4),
+                    scales=w_scales[w][:, cols],
+                    in_=w_grouped[:, cols, :].rearrange("q c t -> q (c t)"),
+                )
+
+        x_quantised = {}
+        grouped_of = {}
+        quantised_of = {}
+        score_of = {}
+        prob_of = {}
+
+        def transpose_and_quantise_x(b):
+            words = x_rows[b][:].bitcast(F32)
+            turned = psum_x.tile([P, PACK, P], F32, name="turned")
+            for c in range(PACK):
+                nc.tensor.transpose(turned[:, c, :], words[:, P * c : P * (c + 1)], identity[:])
+            x_grouped = stage.tile([P, TOKENS * PACK], BF16, name="x_grouped", align_bytes=64)
+            nc.vector.tensor_copy(
+                out=x_grouped[:].bitcast(F32).rearrange("q (r c) -> q r c", c=PACK),
+                in_=turned[:].rearrange("q c r -> q r c"),
+            )
+            x_codes = stage.tile([P, TOKENS], U32, name="x_codes", align_bytes=64)
+            x_scales = stage.tile([P, TOKENS], U8, name="x_scales", align_bytes=64)
+            nc.vector.quantize_mx(out=x_codes[:].bitcast(FP8X4), scales=x_scales[:], in_=x_grouped[:])
+            x_quantised[b] = (x_codes, x_scales)
+
+        def project(unit):
+            b, h = divmod(unit, HEADS)
+            x_codes, x_scales = x_quantised[b]
+            tokens = slice(P * h, P * (h + 1))
+            grouped = stage.tile([P, 2 * HALVES * P * PACK], BF16, name="grouped", align_bytes=64)
+            for w in range(2):
+                for half in range(HALVES):
+                    bank = psum_proj.tile([P, PACK, P], F32, name="bank")
+                    for t in range(PACK):
+                        cols = slice(FEATURES * half + P * t, FEATURES * half + P * (t + 1))
+                        nc.tensor.matmul_mx(
+                            out=bank[:, t, :],
+                            lhsT=w_codes[w][:, cols].bitcast(FP8X4),
+                            lhsT_scale=w_scales[w][:, cols],
+                            rhs=x_codes[:, tokens].bitcast(FP8X4),
+                            rhs_scale=x_scales[:, tokens],
+                            start=True,
+                            stop=True,
+                        )
+                    piece = HALVES * w + half
+                    copy = nc.vector.tensor_copy if piece == 3 else nc.scalar.copy
+                    copy(
+                        out=grouped[:, P * PACK * piece : P * PACK * (piece + 1)].rearrange("p (s t) -> p s t", t=PACK),
+                        in_=bank[:].rearrange("p t s -> p s t"),
+                    )
+            grouped_of[unit] = grouped
+
+        def quantise_and_score(unit):
+            grouped = grouped_of[unit]
+            codes = stage.tile([P, 2 * ROWS], U32, name="codes", align_bytes=64)
+            scales = stage.tile([P, 2 * ROWS], U8, name="scales", align_bytes=64)
+            nc.vector.quantize_mx(out=codes[:].bitcast(FP8X4), scales=scales[:], in_=grouped[:])
+            score = psum_score.tile([P, HALVES, ROWS], F32, name="score")
+            keys = slice(ROWS, 2 * ROWS)
+            for half in range(HALVES):
+                rows = slice(P * half, P * (half + 1))
+                nc.tensor.matmul_mx(
+                    out=score[:, half, :],
+                    lhsT=codes[:, rows].bitcast(FP8X4),
+                    lhsT_scale=scales[:, rows],
+                    rhs=codes[:, keys].bitcast(FP8X4),
+                    rhs_scale=scales[:, keys],
+                    start=True,
+                    stop=True,
+                )
+            score_of[unit] = score
+
+        def exponentials(unit):
+            score = score_of[unit]
+            top = stage.tile([P, HALVES], F32, name="top")
+            nc.vector.tensor_reduce(out=top[:], in_=score[:], axis=mybir.AxisListType.X, op=mybir.AluOpType.max)
+            shift = stage.tile([P, HALVES], F32, name="shift")
+            nc.vector.tensor_scalar_mul(out=shift[:], in0=top[:], scalar1=-SOFTMAX_SCALE)
+            prob = prob_pool.tile([P, HALVES, ROWS], F32, name="prob")
+            total = prob_pool.tile([P, HALVES], F32, name="total")
+            for half in range(HALVES):
+                nc.scalar.activation(
+                    out=prob[:, half, :].rearrange("p (s j) -> p s j", j=HALVES),
+                    in_=score[:, half, :].rearrange("p (j s) -> p s j", j=HALVES),
+                    func=EXP,
+                    bias=shift[:, half : half + 1],
+                    scale=SOFTMAX_SCALE,
+                    accum_out=total[:, half : half + 1],
+                )
+            prob_of[unit] = (prob, total)
+
+        def normalise_and_store(unit):
+            b, h = divmod(unit, HEADS)
+            prob, total = prob_of[unit]
+            inverse = stage.tile([P, HALVES], F32, name="inverse")
+            nc.vector.reciprocal(out=inverse[:], in_=total[:])
+            for half in range(HALVES):
+                nc.vector.tensor_scalar_mul(
+                    out=prob[:, half, :], in0=prob[:, half, :], scalar1=inverse[:, half : half + 1]
+                )
+            nc.sync.dma_start(
+                out=out[b, h].rearrange("(m half) j -> m (half j)", half=HALVES),
+                in_=prob[:].rearrange("p half j -> p (half j)"),
+            )
+
+        transpose_and_quantise_x(0)
+        for step in range(UNITS + 3):
+            if step % HEADS == 0 and step // HEADS + 1 < BATCH:
+                transpose_and_quantise_x(step // HEADS + 1)
+            if step < UNITS:
+                project(step)
+            if 0 <= step - 1 < UNITS:
+                quantise_and_score(step - 1)
+            if 0 <= step - 2 < UNITS:
+                exponentials(step - 2)
+            if 0 <= step - 3 < UNITS:
+                normalise_and_store(step - 3)

@@ -18,6 +18,7 @@ HALVES = 2
 UNITS = BATCH * HEADS
 ROWS = TOKENS
 SOFTMAX_SCALE = 1.0 / math.sqrt(FEATURES)
+W_VECTOR_COLS = 320
 
 FLOPS = 2 * 2 * BATCH * TOKENS * FEATURES * HEADS * FEATURES + 2 * UNITS * ROWS * ROWS * FEATURES
 
@@ -34,26 +35,27 @@ def tile_bertselfattention_pa_t_kernel(tc, x, Wq, Wk, out):
         psum_score = ctx.enter_context(tc.psum_pool(name="psum_score", bufs=2))
 
         weights = (Wq, Wk)
-        w_raw = []
-        x_rows = []
+        w_raw = [keep.tile([P, PACK, HEADS * FEATURES], BF16, name="w_raw%d" % w) for w in range(2)]
         x_view = x.rearrange("b (p two) k -> p b (two k)", two=2)
+        x_rows = []
 
-        def load_weight(w):
-            raw = keep.tile([P, PACK, HEADS * FEATURES], BF16, name="w_raw%d" % w)
-            nc.sync.dma_start(
-                out=raw[:].rearrange("q (u e) c -> q u e c", u=2),
-                in_=weights[w].rearrange("(u q e) c -> q u e c", u=2, e=2),
-            )
-            w_raw.append(raw)
+        def load_weight_half(w, half):
+            cols = slice(FEATURES * half, FEATURES * (half + 1))
+            for u in range(2):
+                nc.sync.dma_start(
+                    out=w_raw[w][:, 2 * u : 2 * u + 2, cols],
+                    in_=weights[w][2 * P * u : 2 * P * (u + 1), cols].rearrange("(q e) c -> q e c", e=2),
+                )
 
         def load_x(b):
             rows = x_pool.tile([P, 2 * FEATURES], BF16, name="x_rows")
             nc.sync.dma_start(out=rows[:], in_=x_view[:, b, :])
             x_rows.append(rows)
 
-        load_weight(0)
         load_x(0)
-        load_weight(1)
+        for half in range(HALVES):
+            for w in range(2):
+                load_weight_half(w, half)
         for b in range(1, BATCH):
             load_x(b)
 
@@ -67,27 +69,39 @@ def tile_bertselfattention_pa_t_kernel(tc, x, Wq, Wk, out):
 
         w_codes = [keep.tile([P, HEADS * FEATURES], U32, name="w_codes%d" % w, align_bytes=64) for w in range(2)]
         w_scales = [keep.tile([P, HEADS * FEATURES], U8, name="w_scales%d" % w, align_bytes=64) for w in range(2)]
-        for w in range(2):
-            w_grouped = keep.tile([P, HEADS * FEATURES, PACK], BF16, name="w_grouped%d" % w, align_bytes=64)
-            for half in range(HALVES):
-                cols = slice(FEATURES * half, FEATURES * (half + 1))
-                copy = nc.vector.tensor_copy if half == 0 else nc.scalar.copy
-                copy(out=w_grouped[:, cols, :], in_=w_raw[w][:, :, cols].rearrange("q t c -> q c t"))
-            for half in range(HALVES):
-                cols = slice(FEATURES * half, FEATURES * (half + 1))
-                nc.vector.quantize_mx(
-                    out=w_codes[w][:, cols].bitcast(FP8X4),
-                    scales=w_scales[w][:, cols],
-                    in_=w_grouped[:, cols, :].rearrange("q c t -> q (c t)"),
-                )
+        w_grouped = [
+            keep.tile([P, HEADS * FEATURES, PACK], BF16, name="w_grouped%d" % w, align_bytes=64) for w in range(2)
+        ]
 
+        def regroup_weight_half(w, half):
+            first = FEATURES * half
+            split = first + W_VECTOR_COLS
+            last = FEATURES * (half + 1)
+            nc.vector.tensor_copy(
+                out=w_grouped[w][:, first:split, :], in_=w_raw[w][:, :, first:split].rearrange("q t c -> q c t")
+            )
+            nc.scalar.copy(
+                out=w_grouped[w][:, split:last, :], in_=w_raw[w][:, :, split:last].rearrange("q t c -> q c t")
+            )
+
+        def quantise_weight_half(w, half):
+            first = FEATURES * half
+            last = FEATURES * (half + 1)
+            nc.vector.quantize_mx(
+                out=w_codes[w][:, first:last].bitcast(FP8X4),
+                scales=w_scales[w][:, first:last],
+                in_=w_grouped[w][:, first:last, :].rearrange("q c t -> q (c t)"),
+            )
+
+        x_grouped_of = {}
         x_quantised = {}
         grouped_of = {}
         quantised_of = {}
+        shift_of = {}
         score_of = {}
         prob_of = {}
 
-        def transpose_and_quantise_x(b):
+        def transpose_x(b):
             words = x_rows[b][:].bitcast(F32)
             turned = psum_x.tile([P, PACK, P], F32, name="turned")
             for c in range(PACK):
@@ -97,6 +111,10 @@ def tile_bertselfattention_pa_t_kernel(tc, x, Wq, Wk, out):
                 out=x_grouped[:].bitcast(F32).rearrange("q (r c) -> q r c", c=PACK),
                 in_=turned[:].rearrange("q c r -> q r c"),
             )
+            x_grouped_of[b] = x_grouped
+
+        def quantise_x(b):
+            x_grouped = x_grouped_of[b]
             x_codes = stage.tile([P, TOKENS], U32, name="x_codes", align_bytes=64)
             x_scales = stage.tile([P, TOKENS], U8, name="x_scales", align_bytes=64)
             nc.vector.quantize_mx(out=x_codes[:].bitcast(FP8X4), scales=x_scales[:], in_=x_grouped[:])
@@ -107,8 +125,8 @@ def tile_bertselfattention_pa_t_kernel(tc, x, Wq, Wk, out):
             x_codes, x_scales = x_quantised[b]
             tokens = slice(P * h, P * (h + 1))
             grouped = stage.tile([P, 2 * HALVES * P * PACK], BF16, name="grouped", align_bytes=64)
-            for w in range(2):
-                for half in range(HALVES):
+            for half in range(HALVES):
+                for w in range(2):
                     bank = psum_proj.tile([P, PACK, P], F32, name="bank")
                     for t in range(PACK):
                         cols = slice(FEATURES * half + P * t, FEATURES * half + P * (t + 1))
@@ -122,18 +140,22 @@ def tile_bertselfattention_pa_t_kernel(tc, x, Wq, Wk, out):
                             stop=True,
                         )
                     piece = HALVES * w + half
-                    copy = nc.vector.tensor_copy if piece == 3 else nc.scalar.copy
+                    copy = nc.vector.tensor_copy if piece == 1 else nc.scalar.copy
                     copy(
                         out=grouped[:, P * PACK * piece : P * PACK * (piece + 1)].rearrange("p (s t) -> p s t", t=PACK),
                         in_=bank[:].rearrange("p t s -> p s t"),
                     )
             grouped_of[unit] = grouped
 
-        def quantise_and_score(unit):
+        def quantise(unit):
             grouped = grouped_of[unit]
             codes = stage.tile([P, 2 * ROWS], U32, name="codes", align_bytes=64)
             scales = stage.tile([P, 2 * ROWS], U8, name="scales", align_bytes=64)
             nc.vector.quantize_mx(out=codes[:].bitcast(FP8X4), scales=scales[:], in_=grouped[:])
+            quantised_of[unit] = (codes, scales)
+
+        def multiply_scores(unit):
+            codes, scales = quantised_of[unit]
             score = psum_score.tile([P, HALVES, ROWS], F32, name="score")
             keys = slice(ROWS, 2 * ROWS)
             for half in range(HALVES):
@@ -149,12 +171,17 @@ def tile_bertselfattention_pa_t_kernel(tc, x, Wq, Wk, out):
                 )
             score_of[unit] = score
 
-        def exponentials(unit):
+        def row_maxima(unit):
             score = score_of[unit]
             top = stage.tile([P, HALVES], F32, name="top")
             nc.vector.tensor_reduce(out=top[:], in_=score[:], axis=mybir.AxisListType.X, op=mybir.AluOpType.max)
             shift = stage.tile([P, HALVES], F32, name="shift")
             nc.vector.tensor_scalar_mul(out=shift[:], in0=top[:], scalar1=-SOFTMAX_SCALE)
+            shift_of[unit] = shift
+
+        def exponentials(unit):
+            score = score_of[unit]
+            shift = shift_of[unit]
             prob = prob_pool.tile([P, HALVES, ROWS], F32, name="prob")
             total = prob_pool.tile([P, HALVES], F32, name="total")
             for half in range(HALVES):
@@ -174,23 +201,42 @@ def tile_bertselfattention_pa_t_kernel(tc, x, Wq, Wk, out):
             inverse = stage.tile([P, HALVES], F32, name="inverse")
             nc.vector.reciprocal(out=inverse[:], in_=total[:])
             for half in range(HALVES):
-                nc.vector.tensor_scalar_mul(
-                    out=prob[:, half, :], in0=prob[:, half, :], scalar1=inverse[:, half : half + 1]
+                nc.gpsimd.tensor_scalar(
+                    out=prob[:, half, :],
+                    in0=prob[:, half, :],
+                    scalar1=inverse[:, half : half + 1],
+                    scalar2=0.0,
+                    op0=mybir.AluOpType.mult,
+                    op1=mybir.AluOpType.add,
                 )
             nc.sync.dma_start(
                 out=out[b, h].rearrange("(m half) j -> m (half j)", half=HALVES),
                 in_=prob[:].rearrange("p half j -> p (half j)"),
             )
 
-        transpose_and_quantise_x(0)
-        for step in range(UNITS + 3):
-            if step % HEADS == 0 and step // HEADS + 1 < BATCH:
-                transpose_and_quantise_x(step // HEADS + 1)
-            if step < UNITS:
-                project(step)
-            if 0 <= step - 1 < UNITS:
-                quantise_and_score(step - 1)
-            if 0 <= step - 2 < UNITS:
-                exponentials(step - 2)
-            if 0 <= step - 3 < UNITS:
-                normalise_and_store(step - 3)
+        with tc.manual_schedule():
+            transpose_x(0)
+            quantise_x(0)
+            for half in range(HALVES):
+                for w in range(2):
+                    regroup_weight_half(w, half)
+                    quantise_weight_half(w, half)
+            for step in range(UNITS + 4):
+                next_batch = step // HEADS + 1
+                new_batch = step % HEADS == 0 and next_batch < BATCH
+                if 0 <= step - 3 < UNITS:
+                    row_maxima(step - 3)
+                if new_batch:
+                    transpose_x(next_batch)
+                if step < UNITS:
+                    project(step)
+                if 0 <= step - 2 < UNITS:
+                    multiply_scores(step - 2)
+                if 0 <= step - 1 < UNITS:
+                    quantise(step - 1)
+                if new_batch:
+                    quantise_x(next_batch)
+                if 0 <= step - 3 < UNITS:
+                    exponentials(step - 3)
+                if 0 <= step - 4 < UNITS:
+                    normalise_and_store(step - 4)

@@ -18,7 +18,7 @@ HALVES = 2
 UNITS = BATCH * HEADS
 ROWS = TOKENS
 SOFTMAX_SCALE = 1.0 / math.sqrt(FEATURES)
-W_VECTOR_COLS = 320
+W_VECTOR_COLS = 256
 
 FLOPS = 2 * 2 * BATCH * TOKENS * FEATURES * HEADS * FEATURES + 2 * UNITS * ROWS * ROWS * FEATURES
 
@@ -52,11 +52,11 @@ def tile_bertselfattention_pa_t_kernel(tc, x, Wq, Wk, out):
             nc.sync.dma_start(out=rows[:], in_=x_view[:, b, :])
             x_rows.append(rows)
 
-        load_x(0)
         for half in range(HALVES):
+            load_x(half)
             for w in range(2):
                 load_weight_half(w, half)
-        for b in range(1, BATCH):
+        for b in range(HALVES, BATCH):
             load_x(b)
 
         identity = keep.tile([P, P], F32, name="identity")
@@ -93,7 +93,9 @@ def tile_bertselfattention_pa_t_kernel(tc, x, Wq, Wk, out):
                 in_=w_grouped[w][:, first:last, :].rearrange("q c t -> q (c t)"),
             )
 
+        turned_of = {}
         x_grouped_of = {}
+        top_of = {}
         x_quantised = {}
         grouped_of = {}
         quantised_of = {}
@@ -106,6 +108,10 @@ def tile_bertselfattention_pa_t_kernel(tc, x, Wq, Wk, out):
             turned = psum_x.tile([P, PACK, P], F32, name="turned")
             for c in range(PACK):
                 nc.tensor.transpose(turned[:, c, :], words[:, P * c : P * (c + 1)], identity[:])
+            turned_of[b] = turned
+
+        def copy_x(b):
+            turned = turned_of[b]
             x_grouped = stage.tile([P, TOKENS * PACK], BF16, name="x_grouped", align_bytes=64)
             nc.vector.tensor_copy(
                 out=x_grouped[:].bitcast(F32).rearrange("q (r c) -> q r c", c=PACK),
@@ -175,6 +181,10 @@ def tile_bertselfattention_pa_t_kernel(tc, x, Wq, Wk, out):
             score = score_of[unit]
             top = stage.tile([P, HALVES], F32, name="top")
             nc.vector.tensor_reduce(out=top[:], in_=score[:], axis=mybir.AxisListType.X, op=mybir.AluOpType.max)
+            top_of[unit] = top
+
+        def scale_maxima(unit):
+            top = top_of[unit]
             shift = stage.tile([P, HALVES], F32, name="shift")
             nc.vector.tensor_scalar_mul(out=shift[:], in0=top[:], scalar1=-SOFTMAX_SCALE)
             shift_of[unit] = shift
@@ -215,27 +225,37 @@ def tile_bertselfattention_pa_t_kernel(tc, x, Wq, Wk, out):
             )
 
         with tc.manual_schedule():
+            chunks = [(w, half) for half in range(HALVES) for w in range(2)]
             transpose_x(0)
+            copy_x(0)
+            regroup_weight_half(*chunks[0])
             quantise_x(0)
-            for half in range(HALVES):
-                for w in range(2):
-                    regroup_weight_half(w, half)
-                    quantise_weight_half(w, half)
+            for before, chunk in zip(chunks, chunks[1:]):
+                regroup_weight_half(*chunk)
+                quantise_weight_half(*before)
+            transpose_x(1)
+            copy_x(1)
+            quantise_weight_half(*chunks[-1])
+            quantise_x(1)
             for step in range(UNITS + 4):
-                next_batch = step // HEADS + 1
-                new_batch = step % HEADS == 0 and next_batch < BATCH
+                turn_batch = step // HEADS + 2 if step % HEADS == 0 else BATCH
+                quantise_batch = step // HEADS + 2 if step % HEADS == 1 else BATCH
                 if 0 <= step - 3 < UNITS:
                     row_maxima(step - 3)
-                if new_batch:
-                    transpose_x(next_batch)
+                if turn_batch < BATCH:
+                    transpose_x(turn_batch)
                 if step < UNITS:
                     project(step)
+                if 0 <= step - 3 < UNITS:
+                    scale_maxima(step - 3)
                 if 0 <= step - 2 < UNITS:
                     multiply_scores(step - 2)
+                if turn_batch < BATCH:
+                    copy_x(turn_batch)
                 if 0 <= step - 1 < UNITS:
                     quantise(step - 1)
-                if new_batch:
-                    quantise_x(next_batch)
+                if quantise_batch < BATCH:
+                    quantise_x(quantise_batch)
                 if 0 <= step - 3 < UNITS:
                     exponentials(step - 3)
                 if 0 <= step - 4 < UNITS:

@@ -19,6 +19,7 @@ UNITS = BATCH * HEADS
 ROWS = TOKENS
 SOFTMAX_SCALE = 1.0 / math.sqrt(FEATURES)
 W_VECTOR_COLS = 256
+RUN = 4
 
 FLOPS = 2 * 2 * BATCH * TOKENS * FEATURES * HEADS * FEATURES + 2 * UNITS * ROWS * ROWS * FEATURES
 
@@ -78,10 +79,12 @@ def tile_bertselfattention_pa_t_kernel(tc, x, Wq, Wk, out):
             split = first + W_VECTOR_COLS
             last = FEATURES * (half + 1)
             nc.vector.tensor_copy(
-                out=w_grouped[w][:, first:split, :], in_=w_raw[w][:, :, first:split].rearrange("q t c -> q c t")
+                out=w_grouped[w][:, first:split, :].rearrange("q (c i) t -> q c t i", i=RUN),
+                in_=w_raw[w][:, :, first:split].rearrange("q t (c i) -> q c t i", i=RUN),
             )
             nc.scalar.copy(
-                out=w_grouped[w][:, split:last, :], in_=w_raw[w][:, :, split:last].rearrange("q t c -> q c t")
+                out=w_grouped[w][:, split:last, :].rearrange("q (c i) t -> q c t i", i=RUN),
+                in_=w_raw[w][:, :, split:last].rearrange("q t (c i) -> q c t i", i=RUN),
             )
 
         def quantise_weight_half(w, half):
@@ -146,7 +149,7 @@ def tile_bertselfattention_pa_t_kernel(tc, x, Wq, Wk, out):
                             stop=True,
                         )
                     piece = HALVES * w + half
-                    copy = nc.vector.tensor_copy if piece == 1 else nc.scalar.copy
+                    copy = nc.vector.tensor_copy if piece == 2 else nc.scalar.copy
                     copy(
                         out=grouped[:, P * PACK * piece : P * PACK * (piece + 1)].rearrange("p (s t) -> p s t", t=PACK),
                         in_=bank[:].rearrange("p t s -> p s t"),
@@ -210,8 +213,9 @@ def tile_bertselfattention_pa_t_kernel(tc, x, Wq, Wk, out):
             prob, total = prob_of[unit]
             inverse = stage.tile([P, HALVES], F32, name="inverse")
             nc.vector.reciprocal(out=inverse[:], in_=total[:])
+            engine = nc.vector if b == BATCH - 1 else nc.gpsimd
             for half in range(HALVES):
-                nc.gpsimd.tensor_scalar(
+                engine.tensor_scalar(
                     out=prob[:, half, :],
                     in0=prob[:, half, :],
                     scalar1=inverse[:, half : half + 1],
@@ -230,13 +234,16 @@ def tile_bertselfattention_pa_t_kernel(tc, x, Wq, Wk, out):
             copy_x(0)
             regroup_weight_half(*chunks[0])
             quantise_x(0)
-            for before, chunk in zip(chunks, chunks[1:]):
-                regroup_weight_half(*chunk)
-                quantise_weight_half(*before)
+            regroup_weight_half(*chunks[1])
+            quantise_weight_half(*chunks[0])
             transpose_x(1)
             copy_x(1)
-            quantise_weight_half(*chunks[-1])
+            regroup_weight_half(*chunks[2])
+            quantise_weight_half(*chunks[1])
             quantise_x(1)
+            regroup_weight_half(*chunks[3])
+            quantise_weight_half(*chunks[2])
+            quantise_weight_half(*chunks[3])
             for step in range(UNITS + 4):
                 turn_batch = step // HEADS + 2 if step % HEADS == 0 else BATCH
                 quantise_batch = step // HEADS + 2 if step % HEADS == 1 else BATCH
@@ -252,11 +259,11 @@ def tile_bertselfattention_pa_t_kernel(tc, x, Wq, Wk, out):
                     multiply_scores(step - 2)
                 if turn_batch < BATCH:
                     copy_x(turn_batch)
+                if 0 <= step - 4 < UNITS:
+                    normalise_and_store(step - 4)
                 if 0 <= step - 1 < UNITS:
                     quantise(step - 1)
                 if quantise_batch < BATCH:
                     quantise_x(quantise_batch)
                 if 0 <= step - 3 < UNITS:
                     exponentials(step - 3)
-                if 0 <= step - 4 < UNITS:
-                    normalise_and_store(step - 4)

import math
from contextlib import ExitStack

import concourse.mybir as mybir
from concourse.masks import make_identity

F32 = mybir.dt.float32
BF16 = mybir.dt.bfloat16
U32 = mybir.dt.uint32
U8 = mybir.dt.uint8
FP8X4 = mybir.dt.float8_e4m3fn_x4
EXP = mybir.ActivationFunctionType.Exp

P = 128
PACK = 4
BATCH, TOKENS, FEATURES, HEADS = 16, 256, 512, 2
HALVES = 2
UNITS = BATCH * HEADS
ROWS = TOKENS
SOFTMAX_SCALE = 1.0 / math.sqrt(FEATURES)
W_VECTOR_COLS = 256
RUN = 4

FLOPS = 2 * 2 * BATCH * TOKENS * FEATURES * HEADS * FEATURES + 2 * UNITS * ROWS * ROWS * FEATURES


def tile_bertselfattention_pa_t_kernel(tc, x, Wq, Wk, out):
    nc = tc.nc
    with ExitStack() as ctx:
        keep = ctx.enter_context(tc.tile_pool(name="keep", bufs=1))
        x_pool = ctx.enter_context(tc.tile_pool(name="x_pool", bufs=BATCH))
        stage = ctx.enter_context(tc.tile_pool(name="stage", bufs=3))
        prob_pool = ctx.enter_context(tc.tile_pool(name="prob_pool", bufs=4))
        psum_x = ctx.enter_context(tc.psum_pool(name="psum_x", bufs=1))
        psum_proj = ctx.enter_context(tc.psum_pool(name="psum_proj", bufs=5))
        psum_score = ctx.enter_context(tc.psum_pool(name="psum_score", bufs=2))

        weights = (Wq, Wk)
        w_raw = [keep.tile([P, PACK, HEADS * FEATURES], BF16, name="w_raw%d" % w) for w in range(2)]
        x_view = x.rearrange("b (p two) k -> p b (two k)", two=2)
        x_rows = []

        def load_weight_half(w, half):
            cols = slice(FEATURES * half, FEATURES * (half + 1))
            for u in range(2):
                nc.sync.dma_start(
                    out=w_raw[w][:, 2 * u : 2 * u + 2, cols],
                    in_=weights[w][2 * P * u : 2 * P * (u + 1), cols].rearrange("(q e) c -> q e c", e=2),
                )

        def load_x(b):
            rows = x_pool.tile([P, 2 * FEATURES], BF16, name="x_rows")
            nc.sync.dma_start(out=rows[:], in_=x_view[:, b, :])
            x_rows.append(rows)

        for half in range(HALVES):
            load_x(half)
            for w in range(2):
                load_weight_half(w, half)
        for b in range(HALVES, BATCH):
            load_x(b)

        identity = keep.tile([P, P], F32, name="identity")
        make_identity(nc, identity[:])

        zero = keep.tile([P, 1], F32, name="zero")
        one = keep.tile([P, 1], F32, name="one")
        nc.vector.memset(zero[:], 0.0)
        nc.scalar.activation(out=one[:], in_=zero[:], func=EXP)

        w_codes = [keep.tile([P, HEADS * FEATURES], U32, name="w_codes%d" % w, align_bytes=64) for w in range(2)]
        w_scales = [keep.tile([P, HEADS * FEATURES], U8, name="w_scales%d" % w, align_bytes=64) for w in range(2)]
        w_grouped = [
            keep.tile([P, HEADS * FEATURES, PACK], BF16, name="w_grouped%d" % w, align_bytes=64) for w in range(2)
        ]

        def regroup_weight_half(w, half):
            first = FEATURES * half
            split = first + W_VECTOR_COLS
            last = FEATURES * (half + 1)
            nc.vector.tensor_copy(
                out=w_grouped[w][:, first:split, :].rearrange("q (c i) t -> q c t i", i=RUN),
                in_=w_raw[w][:, :, first:split].rearrange("q t (c i) -> q c t i", i=RUN),
            )
            nc.scalar.copy(
                out=w_grouped[w][:, split:last, :].rearrange("q (c i) t -> q c t i", i=RUN),
                in_=w_raw[w][:, :, split:last].rearrange("q t (c i) -> q c t i", i=RUN),
            )

        def quantise_weight_half(w, half):
            first = FEATURES * half
            last = FEATURES * (half + 1)
            nc.vector.quantize_mx(
                out=w_codes[w][:, first:last].bitcast(FP8X4),
                scales=w_scales[w][:, first:last],
                in_=w_grouped[w][:, first:last, :].rearrange("q c t -> q (c t)"),
            )

        turned_of = {}
        x_grouped_of = {}
        top_of = {}
        x_quantised = {}
        grouped_of = {}
        quantised_of = {}
        shift_of = {}
        score_of = {}
        prob_of = {}

        def transpose_x(b):
            words = x_rows[b][:].bitcast(F32)
            turned = psum_x.tile([P, PACK, P], F32, name="turned")
            for c in range(PACK):
                nc.tensor.transpose(turned[:, c, :], words[:, P * c : P * (c + 1)], identity[:])
            turned_of[b] = turned

        def copy_x(b):
            turned = turned_of[b]
            x_grouped = stage.tile([P, TOKENS * PACK], BF16, name="x_grouped", align_bytes=64)
            nc.vector.tensor_copy(
                out=x_grouped[:].bitcast(F32).rearrange("q (r c) -> q r c", c=PACK),
                in_=turned[:].rearrange("q c r -> q r c"),
            )
            x_grouped_of[b] = x_grouped

        def quantise_x(b):
            x_grouped = x_grouped_of[b]
            x_codes = stage.tile([P, TOKENS], U32, name="x_codes", align_bytes=64)
            x_scales = stage.tile([P, TOKENS], U8, name="x_scales", align_bytes=64)
            nc.vector.quantize_mx(out=x_codes[:].bitcast(FP8X4), scales=x_scales[:], in_=x_grouped[:])
            x_quantised[b] = (x_codes, x_scales)

        def project(unit):
            b, h = divmod(unit, HEADS)
            x_codes, x_scales = x_quantised[b]
            tokens = slice(P * h, P * (h + 1))
            grouped = stage.tile([P, 2 * HALVES * P * PACK], BF16, name="grouped", align_bytes=64)
            for half in range(HALVES):
                for w in range(2):
                    bank = psum_proj.tile([P, PACK, P], F32, name="bank")
                    for t in range(PACK):
                        cols = slice(FEATURES * half + P * t, FEATURES * half + P * (t + 1))
                        nc.tensor.matmul_mx(
                            out=bank[:, t, :],
                            lhsT=w_codes[w][:, cols].bitcast(FP8X4),
                            lhsT_scale=w_scales[w][:, cols],
                            rhs=x_codes[:, tokens].bitcast(FP8X4),
                            rhs_scale=x_scales[:, tokens],
                            start=True,
                            stop=True,
                        )
                    piece = HALVES * w + half
                    copy = nc.vector.tensor_copy if piece == 2 else nc.scalar.copy
                    copy(
                        out=grouped[:, P * PACK * piece : P * PACK * (piece + 1)].rearrange("p (s t) -> p s t", t=PACK),
                        in_=bank[:].rearrange("p t s -> p s t"),
                    )
            grouped_of[unit] = grouped

        def quantise(unit):
            grouped = grouped_of[unit]
            codes = stage.tile([P, 2 * ROWS], U32, name="codes", align_bytes=64)
            scales = stage.tile([P, 2 * ROWS], U8, name="scales", align_bytes=64)
            nc.vector.quantize_mx(out=codes[:].bitcast(FP8X4), scales=scales[:], in_=grouped[:])
            quantised_of[unit] = (codes, scales)

        def multiply_scores(unit):
            codes, scales = quantised_of[unit]
            score = psum_score.tile([P, HALVES, ROWS], F32, name="score")
            keys = slice(ROWS, 2 * ROWS)
            for half in range(HALVES):
                rows = slice(P * half, P * (half + 1))
                nc.tensor.matmul_mx(
                    out=score[:, half, :],
                    lhsT=codes[:, rows].bitcast(FP8X4),
                    lhsT_scale=scales[:, rows],
                    rhs=codes[:, keys].bitcast(FP8X4),
                    rhs_scale=scales[:, keys],
                    start=True,
                    stop=True,
                )
            score_of[unit] = score

        def row_maxima(unit):
            score = score_of[unit]
            top = stage.tile([P, HALVES], F32, name="top")
            nc.vector.tensor_reduce(out=top[:], in_=score[:], axis=mybir.AxisListType.X, op=mybir.AluOpType.max)
            top_of[unit] = top

        def scale_maxima(unit):
            top = top_of[unit]
            shift = stage.tile([P, HALVES], F32, name="shift")
            nc.vector.tensor_scalar_mul(out=shift[:], in0=top[:], scalar1=-SOFTMAX_SCALE)
            shift_of[unit] = shift

        def exponentials(unit):
            score = score_of[unit]
            shift = shift_of[unit]
            prob = prob_pool.tile([P, HALVES, ROWS], F32, name="prob")
            total = prob_pool.tile([P, HALVES], F32, name="total")
            for half in range(HALVES):
                nc.scalar.activation(
                    out=prob[:, half, :].rearrange("p (s j) -> p s j", j=HALVES),
                    in_=score[:, half, :].rearrange("p (j s) -> p s j", j=HALVES),
                    func=EXP,
                    bias=shift[:, half : half + 1],
                    scale=SOFTMAX_SCALE,
                    accum_out=total[:, half : half + 1],
                )
            prob_of[unit] = (prob, total)

        def normalise_and_store(unit):
            b, h = divmod(unit, HEADS)
            prob, total = prob_of[unit]
            inverse = stage.tile([P, HALVES], F32, name="inverse")
            nc.vector.reciprocal(out=inverse[:], in_=total[:])
            engine = nc.vector if b == BATCH - 1 else nc.gpsimd
            for half in range(HALVES):
                engine.tensor_scalar(
                    out=prob[:, half, :],
                    in0=prob[:, half, :],
                    scalar1=inverse[:, half : half + 1],
                    scalar2=0.0,
                    op0=mybir.AluOpType.mult,
                    op1=mybir.AluOpType.add,
                )
            nc.sync.dma_start(
                out=out[b, h].rearrange("(m half) j -> m (half j)", half=HALVES),
                in_=prob[:].rearrange("p half j -> p (half j)"),
            )

        with tc.manual_schedule():
            chunks = [(w, half) for half in range(HALVES) for w in range(2)]
            transpose_x(0)
            copy_x(0)
            regroup_weight_half(*chunks[0])
            quantise_x(0)
            regroup_weight_half(*chunks[1])
            quantise_weight_half(*chunks[0])
            transpose_x(1)
            copy_x(1)
            regroup_weight_half(*chunks[2])
            quantise_weight_half(*chunks[1])
            quantise_x(1)
            regroup_weight_half(*chunks[3])
            quantise_weight_half(*chunks[2])
            quantise_weight_half(*chunks[3])
            for step in range(UNITS + 4):
                turn_batch = step // HEADS + 2 if step % HEADS == 0 else BATCH
                quantise_batch = step // HEADS + 2 if step % HEADS == 1 else BATCH
                if 0 <= step - 3 < UNITS:
                    row_maxima(step - 3)
                if turn_batch < BATCH:
                    transpose_x(turn_batch)
                if step < UNITS:
                    project(step)
                if 0 <= step - 3 < UNITS:
                    scale_maxima(step - 3)
                if 0 <= step - 2 < UNITS:
                    multiply_scores(step - 2)
                if turn_batch < BATCH:
                    copy_x(turn_batch)
                if 0 <= step - 4 < UNITS:
                    normalise_and_store(step - 4)
                if 0 <= step - 1 < UNITS:
                    quantise(step - 1)
                if quantise_batch < BATCH:
                    quantise_x(quantise_batch)
                if 0 <= step - 3 < UNITS:
                    exponentials(step - 3)
